import numpy as np
import ml_dtypes

BF16 = ml_dtypes.bfloat16


def bf(x):
    return np.asarray(x, np.float32).astype(BF16)


def f32(x):
    return np.asarray(x, np.float32)


def f64(x):
    return np.asarray(x).astype(np.float64)


def striped(idx):
    return np.tile(idx.reshape(-1, 16).T, (8, 1))


C, S, N, B, T, H, DH = 1024, 2048, 1024, 4, 256, 8, 128


def setup_inputs():
    return {"table": f32(np.random.standard_normal((C, S))), "pos": f32(0.5 * np.random.standard_normal((C, T))), "qw": bf(np.random.standard_normal((C, C)) / np.sqrt(C)), "qb": f32(0.3 * np.random.standard_normal((C, 1))), "kw": bf(np.random.standard_normal((C, C)) / np.sqrt(C)), "vw": bf(2.0 * np.random.standard_normal((C, C)) / np.sqrt(C)), "vb": f32(0.2 * np.random.standard_normal((C, 1))), "offs": striped(np.random.permutation(np.tile(np.arange(S), 2))[:N])}


def reference(table, pos, qw, qb, kw, vw, vb, offs):
    idx = offs[:16].T.reshape(-1)
    h = f64(table)[:, idx] + np.tile(f64(pos), (1, B))
    q = f64(qw).T @ h + f64(qb)
    k = f64(kw).T @ h
    v = f64(vw).T @ h + f64(vb)
    att = np.zeros((C, N))
    for b in range(B):
        cols = slice(b * T, (b + 1) * T)
        for a in range(H):
            rows = slice(a * DH, (a + 1) * DH)
            sc = q[rows, cols].T @ k[rows, cols] / np.sqrt(DH)
            e = np.exp(sc - sc.max(axis=1, keepdims=True))
            p = e / e.sum(axis=1, keepdims=True)
            att[rows, cols] = v[rows, cols] @ p.T
    return np.concatenate([h, att], axis=0)

@@ -1,0 +1,226 @@
+import math
+
+import concourse.mybir as mybir
+from concourse.masks import make_identity
+
+BF16, F32, U16 = mybir.dt.bfloat16, mybir.dt.float32, mybir.dt.uint16
+ADD = mybir.AluOpType.add
+EXP = mybir.ActivationFunctionType.Exp
+IDENTITY = mybir.ActivationFunctionType.Identity
+X = mybir.AxisListType.X
+
+P = 128
+CHANNELS, WORDS, TOKENS, SENTENCE, HEADS = 1024, 2048, 1024, 256, 8
+CB = CHANNELS // P
+TB = TOKENS // P
+BANK = 512
+PAIRS = HEADS * 2
+SCALE = 1.0 / math.sqrt(P)
+
+FLOPS = 3 * 2 * CHANNELS * CHANNELS * TOKENS + 2 * 2 * TOKENS * SENTENCE * CHANNELS
+
+
+def tile_transformerclass_b_kernel(tc, table, pos, qw, qb, kw, vw, vb, offs, out):
+    nc = tc.nc
+    with (
+        tc.tile_pool(name="consts", bufs=1) as consts,
+        tc.tile_pool(name="weights", bufs=1) as weights,
+        tc.tile_pool(name="acts", bufs=1) as acts,
+        tc.psum_pool(name="psum", bufs=8) as psum,
+    ):
+        offsets = consts.tile([P, TOKENS // 16], U16, name="offsets")
+        nc.sync.dma_start(offsets[:], offs)
+
+        qw_sb = [weights.tile([P, CB, BANK], BF16, name=f"qw{mh}") for mh in range(2)]
+        kw_sb = [weights.tile([P, CB, BANK], BF16, name=f"kw{mh}") for mh in range(2)]
+        vw_sb = [weights.tile([P, CB, BANK], BF16, name=f"vw{mh}") for mh in range(2)]
+
+        h32 = [acts.tile([P, TOKENS], F32, name=f"h32_{cb}") for cb in range(CB)]
+        h_bf = acts.tile([P, CB, TOKENS], BF16, name="h_bf")
+        q_sb = acts.tile([P, HEADS, TOKENS], BF16, name="q_sb")
+        k_sb = acts.tile([P, HEADS, TOKENS], BF16, name="k_sb")
+        vT_sb = acts.tile([P, TB, CHANNELS], BF16, name="vT_sb")
+
+        vb_all = consts.tile([P, CHANNELS], F32, name="vb_all")
+        nc.scalar.dma_start(vb_all[:], vb.rearrange("c o -> (c o)").partition_broadcast(P))
+
+        ident_bf = consts.tile([P, P], BF16, name="ident_bf")
+        make_identity(nc, ident_bf[:])
+        ident_f32 = consts.tile([P, P], F32, name="ident_f32")
+        make_identity(nc, ident_f32[:])
+        qb_rows = consts.tile([P, P], F32, name="qb_rows")
+        nc.gpsimd.memset(qb_rows[:], 0.0)
+        nc.scalar.dma_start(qb_rows[0:HEADS, :], qb.rearrange("(a p) o -> a (p o)", p=P))
+        qb_bank = psum.tile([P, P], F32, name="qb_bank", tag="bank")
+        nc.tensor.transpose(qb_bank[:], qb_rows[:], ident_f32[:])
+        qb_cols = consts.tile([P, HEADS], F32, name="qb_cols")
+        nc.vector.tensor_copy(qb_cols[:], qb_bank[:, 0:HEADS])
+
+        def load_weights(w_sb, w, mh):
+            nc.sync.dma_start(
+                w_sb[mh][:], w[:, mh * BANK : (mh + 1) * BANK].rearrange("(cb p) m -> p cb m", p=P)
+            )
+
+        def add_vb(t, mh, bank):
+            cols = slice(mh * BANK, (mh + 1) * BANK)
+            nc.vector.tensor_tensor(vT_sb[:, t, cols], bank[:], vb_all[:, cols], ADD)
+
+        with tc.tile_pool(name="lookup", bufs=1) as lookup:
+            table_sb = [lookup.tile([P, WORDS], F32, name=f"table{cb}") for cb in range(CB)]
+            pos_sb = [lookup.tile([P, SENTENCE], F32, name=f"pos{cb}") for cb in range(CB)]
+            for cb in range(CB):
+                rows = slice(cb * P, (cb + 1) * P)
+                nc.sync.dma_start(table_sb[cb][:], table[rows, :])
+                nc.sync.dma_start(pos_sb[cb][:], pos[rows, :])
+                nc.sync.dma_start(vw_sb[0][:, cb, :], vw[rows, 0:BANK])
+            load_weights(qw_sb, qw, 0)
+            load_weights(kw_sb, kw, 0)
+            load_weights(vw_sb, vw, 1)
+            load_weights(qw_sb, qw, 1)
+            load_weights(kw_sb, kw, 1)
+
+            v_banks = [psum.tile([P, BANK], F32, name=f"v_bank{t}", tag="bank") for t in range(TB)]
+            for cb in range(CB):
+                for half in range(2):
+                    for b in (2 * half, 2 * half + 1):
+                        nc.vector.tensor_tensor(
+                            h32[cb][:, b * SENTENCE : (b + 1) * SENTENCE],
+                            table_sb[cb][:].indirect(offsets[:, b * (SENTENCE // 16) : (b + 1) * (SENTENCE // 16)]),
+                            pos_sb[cb][:],
+                            ADD,
+                        )
+                    cols = slice(half * BANK, (half + 1) * BANK)
+                    nc.scalar.copy(h_bf[:, cb, cols], h32[cb][:, cols])
+                nc.sync.dma_start(out[cb * P : (cb + 1) * P, :], h32[cb][:])
+                for t in range(TB):
+                    nc.tensor.matmul(
+                        v_banks[t][:],
+                        lhsT=h_bf[:, cb, t * P : (t + 1) * P],
+                        rhs=vw_sb[0][:, cb, :],
+                        start=(cb == 0),
+                        stop=(cb == CB - 1),
+                    )
+        for t in range(TB):
+            add_vb(t, 0, v_banks[t])
+
+        with (
+            tc.tile_pool(name="work", bufs=2) as work,
+            tc.tile_pool(name="stats", bufs=3) as stats,
+        ):
+
+            def project_v(t, mh):
+                bank = psum.tile([P, BANK], F32, name="v_bank", tag="bank")
+                for cb in range(CB):
+                    nc.tensor.matmul(
+                        bank[:],
+                        lhsT=h_bf[:, cb, t * P : (t + 1) * P],
+                        rhs=vw_sb[mh][:, cb, :],
+                        start=(cb == 0),
+                        stop=(cb == CB - 1),
+                    )
+                add_vb(t, mh, bank)
+
+            def project_head(w_sb, n):
+                a, sp = divmod(n, 2)
+                bank = psum.tile([P, BANK], F32, name="qk_bank", tag="bank")
+                for cb in range(CB):
+                    nc.tensor.matmul(
+                        bank[:],
+                        lhsT=w_sb[a // 4][:, cb, (a % 4) * P : (a % 4 + 1) * P],
+                        rhs=h_bf[:, cb, sp * BANK : (sp + 1) * BANK],
+                        start=(cb == 0),
+                        stop=(cb == CB - 1),
+                    )
+                return bank
+
+            def project_q(n):
+                a, sp = divmod(n, 2)
+                bank = project_head(qw_sb, n)
+                nc.scalar.activation(
+                    q_sb[:, a, sp * BANK : (sp + 1) * BANK], bank[:], IDENTITY, bias=qb_cols[:, a : a + 1]
+                )
+
+            def project_k(n):
+                a, sp = divmod(n, 2)
+                bank = project_head(kw_sb, n)
+                nc.scalar.copy(k_sb[:, a, sp * BANK : (sp + 1) * BANK], bank[:])
+
+            def scores_and_softmax(n):
+                a, sp = divmod(n, 2)
+                e = work.tile([P, 2, 2, SENTENCE], F32, name="e")
+                p = work.tile([P, 2, 2, SENTENCE], BF16, name="p")
+                top = stats.tile([P, 4], F32, name="top")
+                shift = stats.tile([P, 4], F32, name="shift")
+                total = stats.tile([P, 4], F32, name="total")
+                inverse = stats.tile([P, 4], F32, name="inverse")
+                for s in range(2):
+                    first = (2 * sp + s) * SENTENCE
+                    sc = psum.tile([P, 2, SENTENCE], F32, name="sc", tag="bank")
+                    for jb in range(2):
+                        nc.tensor.matmul(
+                            sc[:, jb, :],
+                            lhsT=q_sb[:, a, first + jb * P : first + (jb + 1) * P],
+                            rhs=k_sb[:, a, first : first + SENTENCE],
+                            start=True,
+                            stop=True,
+                        )
+                    both = slice(2 * s, 2 * s + 2)
+                    nc.vector.reduce_max(top[:, both], sc[:], axis=X)
+                    nc.vector.tensor_scalar_mul(shift[:, both], top[:, both], -SCALE)
+                    for jb in range(2):
+                        one = slice(2 * s + jb, 2 * s + jb + 1)
+                        nc.scalar.activation(
+                            e[:, s, jb, :], sc[:, jb, :], EXP, bias=shift[:, one], scale=SCALE, accum_out=total[:, one]
+                        )
+                for s in range(2):
+                    both = slice(2 * s, 2 * s + 2)
+                    nc.vector.reciprocal(inverse[:, both], total[:, both])
+                    for jb in range(2):
+                        one = slice(2 * s + jb, 2 * s + jb + 1)
+                        nc.vector.tensor_scalar_mul(p[:, s, jb, :], e[:, s, jb, :], inverse[:, one])
+                return p
+
+            def flip_weights(p):
+                pT_bank = psum.tile([P, 2, 2, SENTENCE], BF16, name="pT_bank", tag="bank")
+                for s in range(2):
+                    for ib in range(2):
+                        for jb in range(2):
+                            nc.tensor.transpose(
+                                pT_bank[:, s, ib, jb * P : (jb + 1) * P], p[:, s, jb, ib * P : (ib + 1) * P], ident_bf[:]
+                            )
+                pT = work.tile([P, 2, 2, SENTENCE], BF16, name="pT")
+                nc.vector.tensor_copy(pT[:], pT_bank[:])
+                return pT
+
+            def weighted_values(n, pT):
+                a, sp = divmod(n, 2)
+                att_bank = psum.tile([P, BANK], F32, name="att_bank", tag="bank")
+                for s in range(2):
+                    for ib in range(2):
+                        nc.tensor.matmul(
+                            att_bank[:, s * SENTENCE : (s + 1) * SENTENCE],
+                            lhsT=vT_sb[:, 4 * sp + 2 * s + ib, a * P : (a + 1) * P],
+                            rhs=pT[:, s, ib, :],
+                            start=(ib == 0),
+                            stop=(ib == 1),
+                        )
+                att = work.tile([P, BANK], F32, name="att")
+                nc.scalar.copy(att[:], att_bank[:])
+                nc.sync.dma_start(out[CHANNELS + a * P : CHANNELS + (a + 1) * P, sp * BANK : (sp + 1) * BANK], att[:])
+
+            project_q(0)
+            project_k(0)
+            p_tiles, pT_tiles = [], []
+            for n in range(PAIRS + 2):
+                if n + 1 < PAIRS:
+                    project_q(n + 1)
+                if n >= 2:
+                    weighted_values(n - 2, pT_tiles[n - 2])
+                if n < PAIRS:
+                    p_tiles.append(scores_and_softmax(n))
+                if n + 1 < PAIRS:
+                    project_k(n + 1)
+                if n < TB:
+                    project_v(n, 1)
+                if 1 <= n <= PAIRS:
+                    pT_tiles.append(flip_weights(p_tiles[n - 1]))

@@ -41,20 +41,27 @@ def tile_transformerclass_b_kernel(tc, table, pos, qw, qb, kw, vw, vb, offs, out
         k_sb = acts.tile([P, HEADS, TOKENS], BF16, name="k_sb")
         vT_sb = acts.tile([P, TB, CHANNELS], BF16, name="vT_sb")
 
-        vb_all = consts.tile([P, CHANNELS], F32, name="vb_all")
-        nc.scalar.dma_start(vb_all[:], vb.rearrange("c o -> (c o)").partition_broadcast(P))
-
+        qb_rows = consts.tile([HEADS, P], F32, name="qb_rows")
+        nc.sync.dma_start(qb_rows[:], qb.rearrange("(a p) o -> a (p o)", p=P))
+        vb_row = consts.tile([1, CHANNELS], F32, name="vb_row")
+        nc.sync.dma_start(vb_row[:], vb.rearrange("c o -> o c"))
+        ident_heads = consts.tile([HEADS, HEADS], F32, name="ident_heads")
+        make_identity(nc, ident_heads[:])
+        ones_row = consts.tile([1, P], F32, name="ones_row")
+        nc.vector.memset(ones_row[:], 1.0)
         ident_bf = consts.tile([P, P], BF16, name="ident_bf")
         make_identity(nc, ident_bf[:])
-        ident_f32 = consts.tile([P, P], F32, name="ident_f32")
-        make_identity(nc, ident_f32[:])
-        qb_rows = consts.tile([P, P], F32, name="qb_rows")
-        nc.gpsimd.memset(qb_rows[:], 0.0)
-        nc.scalar.dma_start(qb_rows[0:HEADS, :], qb.rearrange("(a p) o -> a (p o)", p=P))
-        qb_bank = psum.tile([P, P], F32, name="qb_bank", tag="bank")
-        nc.tensor.transpose(qb_bank[:], qb_rows[:], ident_f32[:])
+
+        qb_bank = psum.tile([P, HEADS], F32, name="qb_bank", tag="bank")
+        nc.tensor.matmul(qb_bank[:], lhsT=qb_rows[:], rhs=ident_heads[:], start=True, stop=True)
         qb_cols = consts.tile([P, HEADS], F32, name="qb_cols")
-        nc.vector.tensor_copy(qb_cols[:], qb_bank[:, 0:HEADS])
+        nc.scalar.copy(qb_cols[:], qb_bank[:])
+        vb_all = consts.tile([P, CHANNELS], F32, name="vb_all")
+        for mh in range(2):
+            cols = slice(mh * BANK, (mh + 1) * BANK)
+            vb_bank = psum.tile([P, BANK], F32, name="vb_bank", tag="bank")
+            nc.tensor.matmul(vb_bank[:], lhsT=ones_row[:], rhs=vb_row[:, cols], start=True, stop=True)
+            nc.scalar.copy(vb_all[:, cols], vb_bank[:])
 
         def load_weights(w_sb, w, mh):
             nc.sync.dma_start(
@@ -70,8 +77,8 @@ def tile_transformerclass_b_kernel(tc, table, pos, qw, qb, kw, vw, vb, offs, out
             pos_sb = [lookup.tile([P, SENTENCE], F32, name=f"pos{cb}") for cb in range(CB)]
             for cb in range(CB):
                 rows = slice(cb * P, (cb + 1) * P)
-                nc.sync.dma_start(table_sb[cb][:], table[rows, :])
                 nc.sync.dma_start(pos_sb[cb][:], pos[rows, :])
+                nc.sync.dma_start(table_sb[cb][:], table[rows, :])
                 nc.sync.dma_start(vw_sb[0][:, cb, :], vw[rows, 0:BANK])
             load_weights(qw_sb, qw, 0)
             load_weights(kw_sb, kw, 0)
@@ -81,15 +88,14 @@ def tile_transformerclass_b_kernel(tc, table, pos, qw, qb, kw, vw, vb, offs, out
 
             v_banks = [psum.tile([P, BANK], F32, name=f"v_bank{t}", tag="bank") for t in range(TB)]
             for cb in range(CB):
-                for half in range(2):
-                    for b in (2 * half, 2 * half + 1):
-                        nc.vector.tensor_tensor(
-                            h32[cb][:, b * SENTENCE : (b + 1) * SENTENCE],
-                            table_sb[cb][:].indirect(offsets[:, b * (SENTENCE // 16) : (b + 1) * (SENTENCE // 16)]),
-                            pos_sb[cb][:],
-                            ADD,
-                        )
-                    cols = slice(half * BANK, (half + 1) * BANK)
+                for b in range(TOKENS // SENTENCE):
+                    cols = slice(b * SENTENCE, (b + 1) * SENTENCE)
+                    nc.vector.tensor_tensor(
+                        h32[cb][:, cols],
+                        table_sb[cb][:].indirect(offsets[:, b * (SENTENCE // 16) : (b + 1) * (SENTENCE // 16)]),
+                        pos_sb[cb][:],
+                        ADD,
+                    )
                     nc.scalar.copy(h_bf[:, cb, cols], h32[cb][:, cols])
                 nc.sync.dma_start(out[cb * P : (cb + 1) * P, :], h32[cb][:])
                 for t in range(TB):

@@ -82,9 +82,9 @@ def tile_transformerclass_b_kernel(tc, table, pos, qw, qb, kw, vw, vb, offs, out
                 nc.sync.dma_start(vw_sb[0][:, cb, :], vw[rows, 0:BANK])
             load_weights(qw_sb, qw, 0)
             load_weights(kw_sb, kw, 0)
-            load_weights(vw_sb, vw, 1)
             load_weights(qw_sb, qw, 1)
             load_weights(kw_sb, kw, 1)
+            load_weights(vw_sb, vw, 1)
 
             v_banks = [psum.tile([P, BANK], F32, name=f"v_bank{t}", tag="bank") for t in range(TB)]
             for cb in range(CB):
@@ -111,6 +111,7 @@ def tile_transformerclass_b_kernel(tc, table, pos, qw, qb, kw, vw, vb, offs, out
 
         with (
             tc.tile_pool(name="work", bufs=2) as work,
+            tc.tile_pool(name="flipped", bufs=1) as flipped,
             tc.tile_pool(name="stats", bufs=3) as stats,
         ):
 
@@ -186,7 +187,7 @@ def tile_transformerclass_b_kernel(tc, table, pos, qw, qb, kw, vw, vb, offs, out
                         nc.vector.tensor_scalar_mul(p[:, s, jb, :], e[:, s, jb, :], inverse[:, one])
                 return p
 
-            def flip_weights(p):
+            def flip_weights(n, p):
                 pT_bank = psum.tile([P, 2, 2, SENTENCE], BF16, name="pT_bank", tag="bank")
                 for s in range(2):
                     for ib in range(2):
@@ -194,7 +195,7 @@ def tile_transformerclass_b_kernel(tc, table, pos, qw, qb, kw, vw, vb, offs, out
                             nc.tensor.transpose(
                                 pT_bank[:, s, ib, jb * P : (jb + 1) * P], p[:, s, jb, ib * P : (ib + 1) * P], ident_bf[:]
                             )
-                pT = work.tile([P, 2, 2, SENTENCE], BF16, name="pT")
+                pT = flipped.tile([P, 2, 2, SENTENCE], BF16, name=f"pT{n}")
                 nc.vector.tensor_copy(pT[:], pT_bank[:])
                 return pT
 
@@ -217,16 +218,21 @@ def tile_transformerclass_b_kernel(tc, table, pos, qw, qb, kw, vw, vb, offs, out
             project_q(0)
             project_k(0)
             p_tiles, pT_tiles = [], []
-            for n in range(PAIRS + 2):
+            for n in range(PAIRS):
                 if n + 1 < PAIRS:
                     project_q(n + 1)
-                if n >= 2:
+                if 2 <= n < PAIRS // 2 + 2:
                     weighted_values(n - 2, pT_tiles[n - 2])
-                if n < PAIRS:
-                    p_tiles.append(scores_and_softmax(n))
+                p_tiles.append(scores_and_softmax(n))
                 if n + 1 < PAIRS:
                     project_k(n + 1)
-                if n < TB:
-                    project_v(n, 1)
-                if 1 <= n <= PAIRS:
-                    pT_tiles.append(flip_weights(p_tiles[n - 1]))
+                if n >= 1:
+                    pT_tiles.append(flip_weights(n - 1, p_tiles[n - 1]))
+
+            for sp in range(2):
+                for t in range(4 * sp, 4 * sp + 4):
+                    project_v(t, 1)
+                if sp == 0:
+                    pT_tiles.append(flip_weights(PAIRS - 1, p_tiles[PAIRS - 1]))
+                for a in range(HEADS // 2, HEADS):
+                    weighted_values(2 * a + sp, pT_tiles[2 * a + sp])

@@ -11,10 +11,13 @@ X = mybir.AxisListType.X
 
 P = 128
 CHANNELS, WORDS, TOKENS, SENTENCE, HEADS = 1024, 2048, 1024, 256, 8
+BANK = 512
 CB = CHANNELS // P
 TB = TOKENS // P
-BANK = 512
-PAIRS = HEADS * 2
+SB = SENTENCE // P
+PIECE = SENTENCE // 16
+HALF_HEADS = BANK // P
+PAIRS = HEADS * TOKENS // BANK
 SCALE = 1.0 / math.sqrt(P)
 
 FLOPS = 3 * 2 * CHANNELS * CHANNELS * TOKENS + 2 * 2 * TOKENS * SENTENCE * CHANNELS
@@ -68,7 +71,16 @@ def tile_transformerclass_b_kernel(tc, table, pos, qw, qb, kw, vw, vb, offs, out
                 w_sb[mh][:], w[:, mh * BANK : (mh + 1) * BANK].rearrange("(cb p) m -> p cb m", p=P)
             )
 
-        def add_vb(t, mh, bank):
+        def v_matmul(bank, t, mh, cb):
+            nc.tensor.matmul(
+                bank[:],
+                lhsT=h_bf[:, cb, t * P : (t + 1) * P],
+                rhs=vw_sb[mh][:, cb, :],
+                start=(cb == 0),
+                stop=(cb == CB - 1),
+            )
+
+        def add_vb(bank, t, mh):
             cols = slice(mh * BANK, (mh + 1) * BANK)
             nc.vector.tensor_tensor(vT_sb[:, t, cols], bank[:], vb_all[:, cols], ADD)
 
@@ -92,78 +104,68 @@ def tile_transformerclass_b_kernel(tc, table, pos, qw, qb, kw, vw, vb, offs, out
                     cols = slice(b * SENTENCE, (b + 1) * SENTENCE)
                     nc.vector.tensor_tensor(
                         h32[cb][:, cols],
-                        table_sb[cb][:].indirect(offsets[:, b * (SENTENCE // 16) : (b + 1) * (SENTENCE // 16)]),
+                        table_sb[cb][:].indirect(offsets[:, b * PIECE : (b + 1) * PIECE]),
                         pos_sb[cb][:],
                         ADD,
                     )
                     nc.scalar.copy(h_bf[:, cb, cols], h32[cb][:, cols])
                 nc.sync.dma_start(out[cb * P : (cb + 1) * P, :], h32[cb][:])
                 for t in range(TB):
-                    nc.tensor.matmul(
-                        v_banks[t][:],
-                        lhsT=h_bf[:, cb, t * P : (t + 1) * P],
-                        rhs=vw_sb[0][:, cb, :],
-                        start=(cb == 0),
-                        stop=(cb == CB - 1),
-                    )
+                    v_matmul(v_banks[t], t, 0, cb)
         for t in range(TB):
-            add_vb(t, 0, v_banks[t])
+            add_vb(v_banks[t], t, 0)
 
         with (
             tc.tile_pool(name="work", bufs=2) as work,
+            tc.tile_pool(name="stats", bufs=2) as stats,
             tc.tile_pool(name="flipped", bufs=1) as flipped,
-            tc.tile_pool(name="stats", bufs=3) as stats,
+            tc.tile_pool(name="results", bufs=HALF_HEADS) as results,
         ):
 
             def project_v(t, mh):
                 bank = psum.tile([P, BANK], F32, name="v_bank", tag="bank")
                 for cb in range(CB):
-                    nc.tensor.matmul(
-                        bank[:],
-                        lhsT=h_bf[:, cb, t * P : (t + 1) * P],
-                        rhs=vw_sb[mh][:, cb, :],
-                        start=(cb == 0),
-                        stop=(cb == CB - 1),
-                    )
-                add_vb(t, mh, bank)
+                    v_matmul(bank, t, mh, cb)
+                add_vb(bank, t, mh)
 
             def project_head(w_sb, n):
-                a, sp = divmod(n, 2)
-                bank = psum.tile([P, BANK], F32, name="qk_bank", tag="bank")
+                a, half = divmod(n, 2)
+                mh, a_in_half = divmod(a, HALF_HEADS)
+                bank = psum.tile([P, BANK], F32, name="head_bank", tag="bank")
                 for cb in range(CB):
                     nc.tensor.matmul(
                         bank[:],
-                        lhsT=w_sb[a // 4][:, cb, (a % 4) * P : (a % 4 + 1) * P],
-                        rhs=h_bf[:, cb, sp * BANK : (sp + 1) * BANK],
+                        lhsT=w_sb[mh][:, cb, a_in_half * P : (a_in_half + 1) * P],
+                        rhs=h_bf[:, cb, half * BANK : (half + 1) * BANK],
                         start=(cb == 0),
                         stop=(cb == CB - 1),
                     )
                 return bank
 
             def project_q(n):
-                a, sp = divmod(n, 2)
+                a, half = divmod(n, 2)
                 bank = project_head(qw_sb, n)
                 nc.scalar.activation(
-                    q_sb[:, a, sp * BANK : (sp + 1) * BANK], bank[:], IDENTITY, bias=qb_cols[:, a : a + 1]
+                    q_sb[:, a, half * BANK : (half + 1) * BANK], bank[:], IDENTITY, bias=qb_cols[:, a : a + 1]
                 )
 
             def project_k(n):
-                a, sp = divmod(n, 2)
+                a, half = divmod(n, 2)
                 bank = project_head(kw_sb, n)
-                nc.scalar.copy(k_sb[:, a, sp * BANK : (sp + 1) * BANK], bank[:])
+                nc.scalar.copy(k_sb[:, a, half * BANK : (half + 1) * BANK], bank[:])
 
             def scores_and_softmax(n):
-                a, sp = divmod(n, 2)
-                e = work.tile([P, 2, 2, SENTENCE], F32, name="e")
-                p = work.tile([P, 2, 2, SENTENCE], BF16, name="p")
-                top = stats.tile([P, 4], F32, name="top")
-                shift = stats.tile([P, 4], F32, name="shift")
-                total = stats.tile([P, 4], F32, name="total")
-                inverse = stats.tile([P, 4], F32, name="inverse")
+                a, half = divmod(n, 2)
+                e = work.tile([P, 2, SB, SENTENCE], F32, name="e")
+                p = work.tile([P, 2, SB, SENTENCE], BF16, name="p")
+                top = stats.tile([P, 2 * SB], F32, name="top")
+                shift = stats.tile([P, 2 * SB], F32, name="shift")
+                total = stats.tile([P, 2 * SB], F32, name="total")
+                inverse = stats.tile([P, 2 * SB], F32, name="inverse")
                 for s in range(2):
-                    first = (2 * sp + s) * SENTENCE
-                    sc = psum.tile([P, 2, SENTENCE], F32, name="sc", tag="bank")
-                    for jb in range(2):
+                    first = half * BANK + s * SENTENCE
+                    sc = psum.tile([P, SB, SENTENCE], F32, name="sc", tag="bank")
+                    for jb in range(SB):
                         nc.tensor.matmul(
                             sc[:, jb, :],
                             lhsT=q_sb[:, a, first + jb * P : first + (jb + 1) * P],
@@ -171,49 +173,54 @@ def tile_transformerclass_b_kernel(tc, table, pos, qw, qb, kw, vw, vb, offs, out
                             start=True,
                             stop=True,
                         )
-                    both = slice(2 * s, 2 * s + 2)
-                    nc.vector.reduce_max(top[:, both], sc[:], axis=X)
-                    nc.vector.tensor_scalar_mul(shift[:, both], top[:, both], -SCALE)
-                    for jb in range(2):
-                        one = slice(2 * s + jb, 2 * s + jb + 1)
+                    of_s = slice(s * SB, (s + 1) * SB)
+                    nc.vector.reduce_max(top[:, of_s], sc[:], axis=X)
+                    nc.vector.tensor_scalar_mul(shift[:, of_s], top[:, of_s], -SCALE)
+                    for jb in range(SB):
+                        one = slice(s * SB + jb, s * SB + jb + 1)
                         nc.scalar.activation(
                             e[:, s, jb, :], sc[:, jb, :], EXP, bias=shift[:, one], scale=SCALE, accum_out=total[:, one]
                         )
                 for s in range(2):
-                    both = slice(2 * s, 2 * s + 2)
-                    nc.vector.reciprocal(inverse[:, both], total[:, both])
-                    for jb in range(2):
-                        one = slice(2 * s + jb, 2 * s + jb + 1)
+                    of_s = slice(s * SB, (s + 1) * SB)
+                    nc.vector.reciprocal(inverse[:, of_s], total[:, of_s])
+                    for jb in range(SB):
+                        one = slice(s * SB + jb, s * SB + jb + 1)
                         nc.vector.tensor_scalar_mul(p[:, s, jb, :], e[:, s, jb, :], inverse[:, one])
                 return p
 
             def flip_weights(n, p):
-                pT_bank = psum.tile([P, 2, 2, SENTENCE], BF16, name="pT_bank", tag="bank")
+                pT_bank = psum.tile([P, 2, SB, SENTENCE], BF16, name="pT_bank", tag="bank")
                 for s in range(2):
-                    for ib in range(2):
-                        for jb in range(2):
+                    for ib in range(SB):
+                        for jb in range(SB):
                             nc.tensor.transpose(
                                 pT_bank[:, s, ib, jb * P : (jb + 1) * P], p[:, s, jb, ib * P : (ib + 1) * P], ident_bf[:]
                             )
-                pT = flipped.tile([P, 2, 2, SENTENCE], BF16, name=f"pT{n}")
+                pT = flipped.tile([P, 2, SB, SENTENCE], BF16, name=f"pT{n}")
                 nc.vector.tensor_copy(pT[:], pT_bank[:])
                 return pT
 
             def weighted_values(n, pT):
-                a, sp = divmod(n, 2)
+                a, half = divmod(n, 2)
                 att_bank = psum.tile([P, BANK], F32, name="att_bank", tag="bank")
                 for s in range(2):
-                    for ib in range(2):
+                    for ib in range(SB):
                         nc.tensor.matmul(
                             att_bank[:, s * SENTENCE : (s + 1) * SENTENCE],
-                            lhsT=vT_sb[:, 4 * sp + 2 * s + ib, a * P : (a + 1) * P],
+                            lhsT=vT_sb[:, (half * 2 + s) * SB + ib, a * P : (a + 1) * P],
                             rhs=pT[:, s, ib, :],
                             start=(ib == 0),
-                            stop=(ib == 1),
+                            stop=(ib == SB - 1),
                         )
-                att = work.tile([P, BANK], F32, name="att")
-                nc.scalar.copy(att[:], att_bank[:])
-                nc.sync.dma_start(out[CHANNELS + a * P : CHANNELS + (a + 1) * P, sp * BANK : (sp + 1) * BANK], att[:])
+                att = results.tile([P, BANK], F32, name="att")
+                if a % 2 == 0:
+                    nc.scalar.copy(att[:], att_bank[:])
+                else:
+                    nc.vector.tensor_copy(att[:], att_bank[:])
+                nc.sync.dma_start(
+                    out[CHANNELS + a * P : CHANNELS + (a + 1) * P, half * BANK : (half + 1) * BANK], att[:]
+                )
 
             project_q(0)
             project_k(0)
@@ -229,10 +236,10 @@ def tile_transformerclass_b_kernel(tc, table, pos, qw, qb, kw, vw, vb, offs, out
                 if n >= 1:
                     pT_tiles.append(flip_weights(n - 1, p_tiles[n - 1]))
 
-            for sp in range(2):
-                for t in range(4 * sp, 4 * sp + 4):
+            for half in range(2):
+                for t in range(half * 2 * SB, (half + 1) * 2 * SB):
                     project_v(t, 1)
-                if sp == 0:
+                if half == 0:
                     pT_tiles.append(flip_weights(PAIRS - 1, p_tiles[PAIRS - 1]))
-                for a in range(HEADS // 2, HEADS):
-                    weighted_values(2 * a + sp, pT_tiles[2 * a + sp])
+                for a in range(HALF_HEADS, HEADS):
+                    weighted_values(2 * a + half, pT_tiles[2 * a + half])

@@ -122,6 +122,8 @@ def tile_transformerclass_b_kernel(tc, table, pos, qw, qb, kw, vw, vb, offs, out
             tc.tile_pool(name="results", bufs=HALF_HEADS) as results,
         ):
 
+            p_tiles, pT_tiles = [], []
+
             def project_v(t, mh):
                 bank = psum.tile([P, BANK], F32, name="v_bank", tag="bank")
                 for cb in range(CB):
@@ -201,45 +203,46 @@ def tile_transformerclass_b_kernel(tc, table, pos, qw, qb, kw, vw, vb, offs, out
                 nc.vector.tensor_copy(pT[:], pT_bank[:])
                 return pT
 
-            def weighted_values(n, pT):
-                a, half = divmod(n, 2)
-                att_bank = psum.tile([P, BANK], F32, name="att_bank", tag="bank")
-                for s in range(2):
-                    for ib in range(SB):
+            def weighted_values(heads, b):
+                half, s = divmod(b, 2)
+                att_banks = [psum.tile([P, SENTENCE], F32, name=f"att_bank{a}", tag="bank") for a in heads]
+                for ib in range(SB):
+                    for a, att_bank in zip(heads, att_banks):
                         nc.tensor.matmul(
-                            att_bank[:, s * SENTENCE : (s + 1) * SENTENCE],
-                            lhsT=vT_sb[:, (half * 2 + s) * SB + ib, a * P : (a + 1) * P],
-                            rhs=pT[:, s, ib, :],
+                            att_bank[:],
+                            lhsT=vT_sb[:, b * SB + ib, a * P : (a + 1) * P],
+                            rhs=pT_tiles[2 * a + half][:, s, ib, :],
                             start=(ib == 0),
                             stop=(ib == SB - 1),
                         )
-                att = results.tile([P, BANK], F32, name="att")
-                if a % 2 == 0:
-                    nc.scalar.copy(att[:], att_bank[:])
-                else:
-                    nc.vector.tensor_copy(att[:], att_bank[:])
-                nc.sync.dma_start(
-                    out[CHANNELS + a * P : CHANNELS + (a + 1) * P, half * BANK : (half + 1) * BANK], att[:]
-                )
+                for a, att_bank in zip(heads, att_banks):
+                    att = results.tile([P, SENTENCE], F32, name="att")
+                    if a % 2 == 0:
+                        nc.scalar.copy(att[:], att_bank[:])
+                    else:
+                        nc.vector.tensor_copy(att[:], att_bank[:])
+                    nc.sync.dma_start(
+                        out[CHANNELS + a * P : CHANNELS + (a + 1) * P, b * SENTENCE : (b + 1) * SENTENCE], att[:]
+                    )
 
             project_q(0)
             project_k(0)
-            p_tiles, pT_tiles = [], []
             for n in range(PAIRS):
                 if n + 1 < PAIRS:
                     project_q(n + 1)
                 if 2 <= n < PAIRS // 2 + 2:
-                    weighted_values(n - 2, pT_tiles[n - 2])
+                    a, half = divmod(n - 2, 2)
+                    weighted_values([a], 2 * half)
+                    weighted_values([a], 2 * half + 1)
                 p_tiles.append(scores_and_softmax(n))
                 if n + 1 < PAIRS:
                     project_k(n + 1)
                 if n >= 1:
                     pT_tiles.append(flip_weights(n - 1, p_tiles[n - 1]))
 
-            for half in range(2):
-                for t in range(half * 2 * SB, (half + 1) * 2 * SB):
+            for b in range(TOKENS // SENTENCE):
+                for t in range(b * SB, (b + 1) * SB):
                     project_v(t, 1)
-                if half == 0:
+                if b == 0:
                     pT_tiles.append(flip_weights(PAIRS - 1, p_tiles[PAIRS - 1]))
-                for a in range(HALF_HEADS, HEADS):
-                    weighted_values(2 * a + half, pT_tiles[2 * a + half])
+                weighted_values(range(HALF_HEADS, HEADS), b)

@@ -122,18 +122,39 @@ def tile_transformerclass_b_kernel(tc, table, pos, qw, qb, kw, vw, vb, offs, out
             tc.tile_pool(name="results", bufs=HALF_HEADS) as results,
         ):
 
-            p_tiles, pT_tiles = [], []
+            p_tiles, pT_tiles = {}, {}
 
-            def project_v(t, mh):
+            def open_flip(n):
+                return None if n is None else psum.tile([P, 2, SB, SENTENCE], BF16, name="pT_bank", tag="bank")
+
+            def flip_block(n, pT_bank, step):
+                if n is None:
+                    return
+                s, ib, jb = step // (SB * SB), step // SB % SB, step % SB
+                nc.tensor.transpose(
+                    pT_bank[:, s, ib, jb * P : (jb + 1) * P], p_tiles[n][:, s, jb, ib * P : (ib + 1) * P], ident_bf[:]
+                )
+
+            def close_flip(n, pT_bank):
+                if n is None:
+                    return
+                pT_tiles[n] = flipped.tile([P, 2, SB, SENTENCE], BF16, name=f"pT{n}")
+                nc.vector.tensor_copy(pT_tiles[n][:], pT_bank[:])
+
+            def project_v(t, mh, flip=None):
                 bank = psum.tile([P, BANK], F32, name="v_bank", tag="bank")
+                pT_bank = open_flip(flip)
                 for cb in range(CB):
                     v_matmul(bank, t, mh, cb)
+                    flip_block(flip, pT_bank, cb)
                 add_vb(bank, t, mh)
+                close_flip(flip, pT_bank)
 
-            def project_head(w_sb, n):
+            def project_head(w_sb, n, flip=None):
                 a, half = divmod(n, 2)
                 mh, a_in_half = divmod(a, HALF_HEADS)
                 bank = psum.tile([P, BANK], F32, name="head_bank", tag="bank")
+                pT_bank = open_flip(flip)
                 for cb in range(CB):
                     nc.tensor.matmul(
                         bank[:],
@@ -142,11 +163,13 @@ def tile_transformerclass_b_kernel(tc, table, pos, qw, qb, kw, vw, vb, offs, out
                         start=(cb == 0),
                         stop=(cb == CB - 1),
                     )
+                    flip_block(flip, pT_bank, cb)
+                close_flip(flip, pT_bank)
                 return bank
 
-            def project_q(n):
+            def project_q(n, flip=None):
                 a, half = divmod(n, 2)
-                bank = project_head(qw_sb, n)
+                bank = project_head(qw_sb, n, flip)
                 nc.scalar.activation(
                     q_sb[:, a, half * BANK : (half + 1) * BANK], bank[:], IDENTITY, bias=qb_cols[:, a : a + 1]
                 )
@@ -189,19 +212,7 @@ def tile_transformerclass_b_kernel(tc, table, pos, qw, qb, kw, vw, vb, offs, out
                     for jb in range(SB):
                         one = slice(s * SB + jb, s * SB + jb + 1)
                         nc.vector.tensor_scalar_mul(p[:, s, jb, :], e[:, s, jb, :], inverse[:, one])
-                return p
-
-            def flip_weights(n, p):
-                pT_bank = psum.tile([P, 2, SB, SENTENCE], BF16, name="pT_bank", tag="bank")
-                for s in range(2):
-                    for ib in range(SB):
-                        for jb in range(SB):
-                            nc.tensor.transpose(
-                                pT_bank[:, s, ib, jb * P : (jb + 1) * P], p[:, s, jb, ib * P : (ib + 1) * P], ident_bf[:]
-                            )
-                pT = flipped.tile([P, 2, SB, SENTENCE], BF16, name=f"pT{n}")
-                nc.vector.tensor_copy(pT[:], pT_bank[:])
-                return pT
+                p_tiles[n] = p
 
             def weighted_values(heads, b):
                 half, s = divmod(b, 2)
@@ -228,21 +239,26 @@ def tile_transformerclass_b_kernel(tc, table, pos, qw, qb, kw, vw, vb, offs, out
             project_q(0)
             project_k(0)
             for n in range(PAIRS):
+                flip = n - 2 if n >= 2 else None
                 if n + 1 < PAIRS:
-                    project_q(n + 1)
+                    project_q(n + 1, flip)
+                else:
+                    project_v(0, 1, flip)
+                scores_and_softmax(n)
+                if n + 1 < PAIRS:
+                    project_k(n + 1)
                 if 2 <= n < PAIRS // 2 + 2:
                     a, half = divmod(n - 2, 2)
                     weighted_values([a], 2 * half)
                     weighted_values([a], 2 * half + 1)
-                p_tiles.append(scores_and_softmax(n))
-                if n + 1 < PAIRS:
-                    project_k(n + 1)
-                if n >= 1:
-                    pT_tiles.append(flip_weights(n - 1, p_tiles[n - 1]))
 
-            for b in range(TOKENS // SENTENCE):
+            late_heads = range(HALF_HEADS, HEADS)
+            project_v(1, 1, PAIRS - 2)
+            project_v(2, 1)
+            weighted_values(late_heads, 0)
+            project_v(3, 1, PAIRS - 1)
+            weighted_values(late_heads, 1)
+            for b in range(2, TOKENS // SENTENCE):
                 for t in range(b * SB, (b + 1) * SB):
                     project_v(t, 1)
-                if b == 0:
-                    pT_tiles.append(flip_weights(PAIRS - 1, p_tiles[PAIRS - 1]))
-                weighted_values(range(HALF_HEADS, HEADS), b)
+                weighted_values(late_heads, b)

@@ -19,6 +19,8 @@ PIECE = SENTENCE // 16
 HALF_HEADS = BANK // P
 PAIRS = HEADS * TOKENS // BANK
 SCALE = 1.0 / math.sqrt(P)
+EARLY_PAIRS = PAIRS // 2
+EARLY = 3
 
 FLOPS = 3 * 2 * CHANNELS * CHANNELS * TOKENS + 2 * 2 * TOKENS * SENTENCE * CHANNELS
 
@@ -40,9 +42,9 @@ def tile_transformerclass_b_kernel(tc, table, pos, qw, qb, kw, vw, vb, offs, out
 
         h32 = [acts.tile([P, TOKENS], F32, name=f"h32_{cb}") for cb in range(CB)]
         h_bf = acts.tile([P, CB, TOKENS], BF16, name="h_bf")
-        q_sb = acts.tile([P, HEADS, TOKENS], BF16, name="q_sb")
         k_sb = acts.tile([P, HEADS, TOKENS], BF16, name="k_sb")
         vT_sb = acts.tile([P, TB, CHANNELS], BF16, name="vT_sb")
+        k_early = [acts.tile([P, BANK], F32, name=f"k_early{n}") for n in range(EARLY_PAIRS)]
 
         qb_rows = consts.tile([HEADS, P], F32, name="qb_rows")
         nc.sync.dma_start(qb_rows[:], qb.rearrange("(a p) o -> a (p o)", p=P))
@@ -66,9 +68,21 @@ def tile_transformerclass_b_kernel(tc, table, pos, qw, qb, kw, vw, vb, offs, out
             nc.tensor.matmul(vb_bank[:], lhsT=ones_row[:], rhs=vb_row[:, cols], start=True, stop=True)
             nc.scalar.copy(vb_all[:, cols], vb_bank[:])
 
-        def load_weights(w_sb, w, mh):
+        def load_weights(w_sb, w, mh, blocks=slice(0, CB)):
             nc.sync.dma_start(
-                w_sb[mh][:], w[:, mh * BANK : (mh + 1) * BANK].rearrange("(cb p) m -> p cb m", p=P)
+                w_sb[mh][:, blocks, :],
+                w[blocks.start * P : blocks.stop * P, mh * BANK : (mh + 1) * BANK].rearrange("(cb p) m -> p cb m", p=P),
+            )
+
+        def head_matmul(bank, w_sb, n, cb, blocks):
+            a, half = divmod(n, 2)
+            mh, a_in_half = divmod(a, HALF_HEADS)
+            nc.tensor.matmul(
+                bank[:],
+                lhsT=w_sb[mh][:, cb, a_in_half * P : (a_in_half + 1) * P],
+                rhs=h_bf[:, cb, half * BANK : (half + 1) * BANK],
+                start=(cb == blocks[0]),
+                stop=(cb == blocks[-1]),
             )
 
         def v_matmul(bank, t, mh, cb):
@@ -91,14 +105,21 @@ def tile_transformerclass_b_kernel(tc, table, pos, qw, qb, kw, vw, vb, offs, out
                 rows = slice(cb * P, (cb + 1) * P)
                 nc.sync.dma_start(pos_sb[cb][:], pos[rows, :])
                 nc.sync.dma_start(table_sb[cb][:], table[rows, :])
-                nc.sync.dma_start(vw_sb[0][:, cb, :], vw[rows, 0:BANK])
+                if cb < EARLY:
+                    load_weights(kw_sb, kw, 0, slice(cb, cb + 1))
+                else:
+                    load_weights(vw_sb, vw, 0, slice(cb, cb + 1))
+                if cb == EARLY - 1:
+                    load_weights(vw_sb, vw, 0, slice(0, EARLY))
             load_weights(qw_sb, qw, 0)
-            load_weights(kw_sb, kw, 0)
+            load_weights(kw_sb, kw, 0, slice(EARLY, CB))
             load_weights(qw_sb, qw, 1)
             load_weights(kw_sb, kw, 1)
             load_weights(vw_sb, vw, 1)
 
-            v_banks = [psum.tile([P, BANK], F32, name=f"v_bank{t}", tag="bank") for t in range(TB)]
+            early_pairs = [2 * a + half for half in range(2) for a in range(HALF_HEADS)]
+            k_banks = {n: psum.tile([P, BANK], F32, name=f"k_bank{n}", tag="bank") for n in early_pairs}
+            v_banks = []
             for cb in range(CB):
                 for b in range(TOKENS // SENTENCE):
                     cols = slice(b * SENTENCE, (b + 1) * SENTENCE)
@@ -110,8 +131,19 @@ def tile_transformerclass_b_kernel(tc, table, pos, qw, qb, kw, vw, vb, offs, out
                     )
                     nc.scalar.copy(h_bf[:, cb, cols], h32[cb][:, cols])
                 nc.sync.dma_start(out[cb * P : (cb + 1) * P, :], h32[cb][:])
-                for t in range(TB):
-                    v_matmul(v_banks[t], t, 0, cb)
+                if cb < EARLY:
+                    for n in early_pairs:
+                        head_matmul(k_banks[n], kw_sb, n, cb, range(EARLY))
+                else:
+                    for t in range(TB):
+                        v_matmul(v_banks[t], t, 0, cb)
+                if cb == EARLY - 1:
+                    for n in early_pairs:
+                        nc.scalar.copy(k_early[n][:], k_banks[n][:])
+                    for t in range(TB):
+                        v_banks.append(psum.tile([P, BANK], F32, name=f"v_bank{t}", tag="bank"))
+                        for behind in range(EARLY):
+                            v_matmul(v_banks[t], t, 0, behind)
         for t in range(TB):
             add_vb(v_banks[t], t, 0)
 
@@ -120,7 +152,9 @@ def tile_transformerclass_b_kernel(tc, table, pos, qw, qb, kw, vw, vb, offs, out
             tc.tile_pool(name="stats", bufs=2) as stats,
             tc.tile_pool(name="flipped", bufs=1) as flipped,
             tc.tile_pool(name="results", bufs=HALF_HEADS) as results,
+            tc.tile_pool(name="queries", bufs=1) as queries,
         ):
+            q_sb = queries.tile([P, HEADS, TOKENS], BF16, name="q_sb")
 
             p_tiles, pT_tiles = {}, {}
 
@@ -150,34 +184,29 @@ def tile_transformerclass_b_kernel(tc, table, pos, qw, qb, kw, vw, vb, offs, out
                 add_vb(bank, t, mh)
                 close_flip(flip, pT_bank)
 
-            def project_head(w_sb, n, flip=None):
-                a, half = divmod(n, 2)
-                mh, a_in_half = divmod(a, HALF_HEADS)
-                bank = psum.tile([P, BANK], F32, name="head_bank", tag="bank")
-                pT_bank = open_flip(flip)
-                for cb in range(CB):
-                    nc.tensor.matmul(
-                        bank[:],
-                        lhsT=w_sb[mh][:, cb, a_in_half * P : (a_in_half + 1) * P],
-                        rhs=h_bf[:, cb, half * BANK : (half + 1) * BANK],
-                        start=(cb == 0),
-                        stop=(cb == CB - 1),
-                    )
-                    flip_block(flip, pT_bank, cb)
-                close_flip(flip, pT_bank)
-                return bank
-
             def project_q(n, flip=None):
                 a, half = divmod(n, 2)
-                bank = project_head(qw_sb, n, flip)
+                bank = psum.tile([P, BANK], F32, name="q_bank", tag="bank")
+                pT_bank = open_flip(flip)
+                for cb in range(CB):
+                    head_matmul(bank, qw_sb, n, cb, range(CB))
+                    flip_block(flip, pT_bank, cb)
+                close_flip(flip, pT_bank)
                 nc.scalar.activation(
                     q_sb[:, a, half * BANK : (half + 1) * BANK], bank[:], IDENTITY, bias=qb_cols[:, a : a + 1]
                 )
 
             def project_k(n):
                 a, half = divmod(n, 2)
-                bank = project_head(kw_sb, n)
-                nc.scalar.copy(k_sb[:, a, half * BANK : (half + 1) * BANK], bank[:])
+                k_cols = k_sb[:, a, half * BANK : (half + 1) * BANK]
+                bank = psum.tile([P, BANK], F32, name="k_bank", tag="bank")
+                blocks = range(EARLY, CB) if n < EARLY_PAIRS else range(CB)
+                for cb in blocks:
+                    head_matmul(bank, kw_sb, n, cb, blocks)
+                if n < EARLY_PAIRS:
+                    nc.vector.tensor_tensor(k_cols, bank[:], k_early[n][:], ADD)
+                else:
+                    nc.scalar.copy(k_cols, bank[:])
 
             def scores_and_softmax(n):
                 a, half = divmod(n, 2)

@@ -48,12 +48,8 @@ def tile_transformerclass_b_kernel(tc, table, pos, qw, qb, kw, vw, vb, offs, out
 
         qb_rows = consts.tile([HEADS, P], F32, name="qb_rows")
         nc.sync.dma_start(qb_rows[:], qb.rearrange("(a p) o -> a (p o)", p=P))
-        vb_row = consts.tile([1, CHANNELS], F32, name="vb_row")
-        nc.sync.dma_start(vb_row[:], vb.rearrange("c o -> o c"))
         ident_heads = consts.tile([HEADS, HEADS], F32, name="ident_heads")
         make_identity(nc, ident_heads[:])
-        ones_row = consts.tile([1, P], F32, name="ones_row")
-        nc.vector.memset(ones_row[:], 1.0)
         ident_bf = consts.tile([P, P], BF16, name="ident_bf")
         make_identity(nc, ident_bf[:])
 
@@ -62,11 +58,6 @@ def tile_transformerclass_b_kernel(tc, table, pos, qw, qb, kw, vw, vb, offs, out
         qb_cols = consts.tile([P, HEADS], F32, name="qb_cols")
         nc.scalar.copy(qb_cols[:], qb_bank[:])
         vb_all = consts.tile([P, CHANNELS], F32, name="vb_all")
-        for mh in range(2):
-            cols = slice(mh * BANK, (mh + 1) * BANK)
-            vb_bank = psum.tile([P, BANK], F32, name="vb_bank", tag="bank")
-            nc.tensor.matmul(vb_bank[:], lhsT=ones_row[:], rhs=vb_row[:, cols], start=True, stop=True)
-            nc.scalar.copy(vb_all[:, cols], vb_bank[:])
 
         def load_weights(w_sb, w, mh, blocks=slice(0, CB)):
             nc.sync.dma_start(
@@ -111,6 +102,7 @@ def tile_transformerclass_b_kernel(tc, table, pos, qw, qb, kw, vw, vb, offs, out
                     load_weights(vw_sb, vw, 0, slice(cb, cb + 1))
                 if cb == EARLY - 1:
                     load_weights(vw_sb, vw, 0, slice(0, EARLY))
+                    nc.sync.dma_start(vb_all[:], vb.rearrange("c o -> (o c)").partition_broadcast(P))
             load_weights(qw_sb, qw, 0)
             load_weights(kw_sb, kw, 0, slice(EARLY, CB))
             load_weights(qw_sb, qw, 1)
@@ -119,6 +111,17 @@ def tile_transformerclass_b_kernel(tc, table, pos, qw, qb, kw, vw, vb, offs, out
 
             early_pairs = [2 * a + half for half in range(2) for a in range(HALF_HEADS)]
             k_banks = {n: psum.tile([P, BANK], F32, name=f"k_bank{n}", tag="bank") for n in early_pairs}
+
+            def early_matmul(a, b, cb):
+                half, s = divmod(b, 2)
+                nc.tensor.matmul(
+                    k_banks[2 * a + half][:, s * SENTENCE : (s + 1) * SENTENCE],
+                    lhsT=kw_sb[0][:, cb, a * P : (a + 1) * P],
+                    rhs=h_bf[:, cb, b * SENTENCE : (b + 1) * SENTENCE],
+                    start=(cb == 0 and s == 0),
+                    stop=(cb == EARLY - 1 and s == 1),
+                )
+
             v_banks = []
             for cb in range(CB):
                 for b in range(TOKENS // SENTENCE):
@@ -132,8 +135,9 @@ def tile_transformerclass_b_kernel(tc, table, pos, qw, qb, kw, vw, vb, offs, out
                     nc.scalar.copy(h_bf[:, cb, cols], h32[cb][:, cols])
                 nc.sync.dma_start(out[cb * P : (cb + 1) * P, :], h32[cb][:])
                 if cb < EARLY:
-                    for n in early_pairs:
-                        head_matmul(k_banks[n], kw_sb, n, cb, range(EARLY))
+                    for b in range(TOKENS // SENTENCE):
+                        for a in range(HALF_HEADS):
+                            early_matmul(a, b, cb)
                 else:
                     for t in range(TB):
                         v_matmul(v_banks[t], t, 0, cb)

@@ -48,6 +48,10 @@ def tile_transformerclass_b_kernel(tc, table, pos, qw, qb, kw, vw, vb, offs, out
 
         qb_rows = consts.tile([HEADS, P], F32, name="qb_rows")
         nc.sync.dma_start(qb_rows[:], qb.rearrange("(a p) o -> a (p o)", p=P))
+        vb_row = consts.tile([1, BANK], F32, name="vb_row")
+        nc.sync.dma_start(vb_row[:], vb[0:BANK, :].rearrange("c o -> o c"))
+        ones_row = consts.tile([1, P], F32, name="ones_row")
+        nc.vector.memset(ones_row[:], 1.0)
         ident_heads = consts.tile([HEADS, HEADS], F32, name="ident_heads")
         make_identity(nc, ident_heads[:])
         ident_bf = consts.tile([P, P], BF16, name="ident_bf")
@@ -58,6 +62,9 @@ def tile_transformerclass_b_kernel(tc, table, pos, qw, qb, kw, vw, vb, offs, out
         qb_cols = consts.tile([P, HEADS], F32, name="qb_cols")
         nc.scalar.copy(qb_cols[:], qb_bank[:])
         vb_all = consts.tile([P, CHANNELS], F32, name="vb_all")
+        vb_bank = psum.tile([P, BANK], F32, name="vb_bank", tag="bank")
+        nc.tensor.matmul(vb_bank[:], lhsT=ones_row[:], rhs=vb_row[:], start=True, stop=True)
+        nc.scalar.copy(vb_all[:, 0:BANK], vb_bank[:])
 
         def load_weights(w_sb, w, mh, blocks=slice(0, CB)):
             nc.sync.dma_start(
@@ -102,12 +109,12 @@ def tile_transformerclass_b_kernel(tc, table, pos, qw, qb, kw, vw, vb, offs, out
                     load_weights(vw_sb, vw, 0, slice(cb, cb + 1))
                 if cb == EARLY - 1:
                     load_weights(vw_sb, vw, 0, slice(0, EARLY))
-                    nc.sync.dma_start(vb_all[:], vb.rearrange("c o -> (o c)").partition_broadcast(P))
             load_weights(qw_sb, qw, 0)
             load_weights(kw_sb, kw, 0, slice(EARLY, CB))
             load_weights(qw_sb, qw, 1)
             load_weights(kw_sb, kw, 1)
             load_weights(vw_sb, vw, 1)
+            nc.sync.dma_start(vb_all[:, BANK:], vb[BANK:, :].rearrange("c o -> (o c)").partition_broadcast(P))
 
             early_pairs = [2 * a + half for half in range(2) for a in range(HALF_HEADS)]
             k_banks = {n: psum.tile([P, BANK], F32, name=f"k_bank{n}", tag="bank") for n in early_pairs}

@@ -162,7 +162,7 @@ def tile_transformerclass_b_kernel(tc, table, pos, qw, qb, kw, vw, vb, offs, out
             tc.tile_pool(name="work", bufs=2) as work,
             tc.tile_pool(name="stats", bufs=2) as stats,
             tc.tile_pool(name="flipped", bufs=1) as flipped,
-            tc.tile_pool(name="results", bufs=HALF_HEADS) as results,
+            tc.tile_pool(name="results", bufs=2 * HALF_HEADS) as results,
             tc.tile_pool(name="queries", bufs=1) as queries,
         ):
             q_sb = queries.tile([P, HEADS, TOKENS], BF16, name="q_sb")
@@ -297,8 +297,10 @@ def tile_transformerclass_b_kernel(tc, table, pos, qw, qb, kw, vw, vb, offs, out
             project_v(2, 1)
             weighted_values(late_heads, 0)
             project_v(3, 1, PAIRS - 1)
+            project_v(4, 1)
             weighted_values(late_heads, 1)
-            for b in range(2, TOKENS // SENTENCE):
-                for t in range(b * SB, (b + 1) * SB):
-                    project_v(t, 1)
-                weighted_values(late_heads, b)
+            project_v(5, 1)
+            project_v(6, 1)
+            project_v(7, 1)
+            weighted_values(late_heads, 2)
+            weighted_values(late_heads, 3)

@@ -184,7 +184,7 @@ def tile_transformerclass_b_kernel(tc, table, pos, qw, qb, kw, vw, vb, offs, out
                 if n is None:
                     return
                 pT_tiles[n] = flipped.tile([P, 2, SB, SENTENCE], BF16, name=f"pT{n}")
-                nc.vector.tensor_copy(pT_tiles[n][:], pT_bank[:])
+                nc.scalar.copy(pT_tiles[n][:], pT_bank[:])
 
             def project_v(t, mh, flip=None):
                 bank = psum.tile([P, BANK], F32, name="v_bank", tag="bank")

@@ -15,7 +15,11 @@ BANK = 512
 CB = CHANNELS // P
 TB = TOKENS // P
 SB = SENTENCE // P
-PIECE = SENTENCE // 16
+TO_A_COLUMN = 16
+PIECES = [slice(b * SENTENCE, (b + 1) * SENTENCE) for b in range(TOKENS // SENTENCE - 1)] + [
+    slice(TOKENS - SENTENCE, TOKENS - P),
+    slice(TOKENS - P, TOKENS),
+]
 HALF_HEADS = BANK // P
 PAIRS = HEADS * TOKENS // BANK
 SCALE = 1.0 / math.sqrt(P)
@@ -119,32 +123,32 @@ def tile_transformerclass_b_kernel(tc, table, pos, qw, qb, kw, vw, vb, offs, out
             early_pairs = [2 * a + half for half in range(2) for a in range(HALF_HEADS)]
             k_banks = {n: psum.tile([P, BANK], F32, name=f"k_bank{n}", tag="bank") for n in early_pairs}
 
-            def early_matmul(a, b, cb):
-                half, s = divmod(b, 2)
+            def early_matmul(a, cols, cb):
+                half = cols.start // BANK
                 nc.tensor.matmul(
-                    k_banks[2 * a + half][:, s * SENTENCE : (s + 1) * SENTENCE],
+                    k_banks[2 * a + half][:, cols.start - half * BANK : cols.stop - half * BANK],
                     lhsT=kw_sb[0][:, cb, a * P : (a + 1) * P],
-                    rhs=h_bf[:, cb, b * SENTENCE : (b + 1) * SENTENCE],
-                    start=(cb == 0 and s == 0),
-                    stop=(cb == EARLY - 1 and s == 1),
+                    rhs=h_bf[:, cb, cols],
+                    start=(cb == 0 and cols.start % BANK == 0),
+                    stop=(cb == EARLY - 1 and cols.stop % BANK == 0),
                 )
 
             v_banks = []
             for cb in range(CB):
-                for b in range(TOKENS // SENTENCE):
-                    cols = slice(b * SENTENCE, (b + 1) * SENTENCE)
+                for cols in PIECES:
+                    in_sentence = cols.start % SENTENCE
                     nc.vector.tensor_tensor(
                         h32[cb][:, cols],
-                        table_sb[cb][:].indirect(offsets[:, b * PIECE : (b + 1) * PIECE]),
-                        pos_sb[cb][:],
+                        table_sb[cb][:].indirect(offsets[:, cols.start // TO_A_COLUMN : cols.stop // TO_A_COLUMN]),
+                        pos_sb[cb][:, in_sentence : in_sentence + cols.stop - cols.start],
                         ADD,
                     )
                     nc.scalar.copy(h_bf[:, cb, cols], h32[cb][:, cols])
                 nc.sync.dma_start(out[cb * P : (cb + 1) * P, :], h32[cb][:])
                 if cb < EARLY:
-                    for b in range(TOKENS // SENTENCE):
+                    for cols in PIECES:
                         for a in range(HALF_HEADS):
-                            early_matmul(a, b, cb)
+                            early_matmul(a, cols, cb)
                 else:
                     for t in range(TB):
                         v_matmul(v_banks[t], t, 0, cb)

@@ -153,7 +153,9 @@ def tile_transformerclass_b_kernel(tc, table, pos, qw, qb, kw, vw, vb, offs, out
                     for t in range(TB):
                         v_matmul(v_banks[t], t, 0, cb)
                 if cb == EARLY - 1:
-                    for n in early_pairs:
+                    for n in early_pairs[:2]:
+                        nc.vector.tensor_copy(k_early[n][:], k_banks[n][:])
+                    for n in early_pairs[2:]:
                         nc.scalar.copy(k_early[n][:], k_banks[n][:])
                     for t in range(TB):
                         v_banks.append(psum.tile([P, BANK], F32, name=f"v_bank{t}", tag="bank"))

import math

import concourse.mybir as mybir
from concourse.masks import make_identity

BF16, F32, U16 = mybir.dt.bfloat16, mybir.dt.float32, mybir.dt.uint16
ADD = mybir.AluOpType.add
EXP = mybir.ActivationFunctionType.Exp
IDENTITY = mybir.ActivationFunctionType.Identity
X = mybir.AxisListType.X

P = 128
CHANNELS, WORDS, TOKENS, SENTENCE, HEADS = 1024, 2048, 1024, 256, 8
BANK = 512
CB = CHANNELS // P
TB = TOKENS // P
SB = SENTENCE // P
TO_A_COLUMN = 16
PIECES = [slice(b * SENTENCE, (b + 1) * SENTENCE) for b in range(TOKENS // SENTENCE - 1)] + [
    slice(TOKENS - SENTENCE, TOKENS - P),
    slice(TOKENS - P, TOKENS),
]
HALF_HEADS = BANK // P
PAIRS = HEADS * TOKENS // BANK
SCALE = 1.0 / math.sqrt(P)
EARLY_PAIRS = PAIRS // 2
EARLY = 3

FLOPS = 3 * 2 * CHANNELS * CHANNELS * TOKENS + 2 * 2 * TOKENS * SENTENCE * CHANNELS


def tile_transformerclass_b_kernel(tc, table, pos, qw, qb, kw, vw, vb, offs, out):
    nc = tc.nc
    with (
        tc.tile_pool(name="consts", bufs=1) as consts,
        tc.tile_pool(name="weights", bufs=1) as weights,
        tc.tile_pool(name="acts", bufs=1) as acts,
        tc.psum_pool(name="psum", bufs=8) as psum,
    ):
        offsets = consts.tile([P, TOKENS // 16], U16, name="offsets")
        nc.sync.dma_start(offsets[:], offs)

        qw_sb = [weights.tile([P, CB, BANK], BF16, name=f"qw{mh}") for mh in range(2)]
        kw_sb = [weights.tile([P, CB, BANK], BF16, name=f"kw{mh}") for mh in range(2)]
        vw_sb = [weights.tile([P, CB, BANK], BF16, name=f"vw{mh}") for mh in range(2)]

        h32 = [acts.tile([P, TOKENS], F32, name=f"h32_{cb}") for cb in range(CB)]
        h_bf = acts.tile([P, CB, TOKENS], BF16, name="h_bf")
        k_sb = acts.tile([P, HEADS, TOKENS], BF16, name="k_sb")
        vT_sb = acts.tile([P, TB, CHANNELS], BF16, name="vT_sb")
        k_early = [acts.tile([P, BANK], F32, name=f"k_early{n}") for n in range(EARLY_PAIRS)]

        qb_rows = consts.tile([HEADS, P], F32, name="qb_rows")
        nc.sync.dma_start(qb_rows[:], qb.rearrange("(a p) o -> a (p o)", p=P))
        vb_row = consts.tile([1, BANK], F32, name="vb_row")
        nc.sync.dma_start(vb_row[:], vb[0:BANK, :].rearrange("c o -> o c"))
        ones_row = consts.tile([1, P], F32, name="ones_row")
        nc.vector.memset(ones_row[:], 1.0)
        ident_heads = consts.tile([HEADS, HEADS], F32, name="ident_heads")
        make_identity(nc, ident_heads[:])
        ident_bf = consts.tile([P, P], BF16, name="ident_bf")
        make_identity(nc, ident_bf[:])

        qb_bank = psum.tile([P, HEADS], F32, name="qb_bank", tag="bank")
        nc.tensor.matmul(qb_bank[:], lhsT=qb_rows[:], rhs=ident_heads[:], start=True, stop=True)
        qb_cols = consts.tile([P, HEADS], F32, name="qb_cols")
        nc.scalar.copy(qb_cols[:], qb_bank[:])
        vb_all = consts.tile([P, CHANNELS], F32, name="vb_all")
        vb_bank = psum.tile([P, BANK], F32, name="vb_bank", tag="bank")
        nc.tensor.matmul(vb_bank[:], lhsT=ones_row[:], rhs=vb_row[:], start=True, stop=True)
        nc.scalar.copy(vb_all[:, 0:BANK], vb_bank[:])

        def load_weights(w_sb, w, mh, blocks=slice(0, CB)):
            nc.sync.dma_start(
                w_sb[mh][:, blocks, :],
                w[blocks.start * P : blocks.stop * P, mh * BANK : (mh + 1) * BANK].rearrange("(cb p) m -> p cb m", p=P),
            )

        def head_matmul(bank, w_sb, n, cb, blocks):
            a, half = divmod(n, 2)
            mh, a_in_half = divmod(a, HALF_HEADS)
            nc.tensor.matmul(
                bank[:],
                lhsT=w_sb[mh][:, cb, a_in_half * P : (a_in_half + 1) * P],
                rhs=h_bf[:, cb, half * BANK : (half + 1) * BANK],
                start=(cb == blocks[0]),
                stop=(cb == blocks[-1]),
            )

        def v_matmul(bank, t, mh, cb):
            nc.tensor.matmul(
                bank[:],
                lhsT=h_bf[:, cb, t * P : (t + 1) * P],
                rhs=vw_sb[mh][:, cb, :],
                start=(cb == 0),
                stop=(cb == CB - 1),
            )

        def add_vb(bank, t, mh):
            cols = slice(mh * BANK, (mh + 1) * BANK)
            nc.vector.tensor_tensor(vT_sb[:, t, cols], bank[:], vb_all[:, cols], ADD)

        with tc.tile_pool(name="lookup", bufs=1) as lookup:
            table_sb = [lookup.tile([P, WORDS], F32, name=f"table{cb}") for cb in range(CB)]
            pos_sb = [lookup.tile([P, SENTENCE], F32, name=f"pos{cb}") for cb in range(CB)]
            for cb in range(CB):
                rows = slice(cb * P, (cb + 1) * P)
                nc.sync.dma_start(pos_sb[cb][:], pos[rows, :])
                nc.sync.dma_start(table_sb[cb][:], table[rows, :])
                if cb < EARLY:
                    load_weights(kw_sb, kw, 0, slice(cb, cb + 1))
                else:
                    load_weights(vw_sb, vw, 0, slice(cb, cb + 1))
                if cb == EARLY - 1:
                    load_weights(vw_sb, vw, 0, slice(0, EARLY))
            load_weights(qw_sb, qw, 0)
            load_weights(kw_sb, kw, 0, slice(EARLY, CB))
            load_weights(qw_sb, qw, 1)
            load_weights(kw_sb, kw, 1)
            load_weights(vw_sb, vw, 1)
            nc.sync.dma_start(vb_all[:, BANK:], vb[BANK:, :].rearrange("c o -> (o c)").partition_broadcast(P))

            early_pairs = [2 * a + half for half in range(2) for a in range(HALF_HEADS)]
            k_banks = {n: psum.tile([P, BANK], F32, name=f"k_bank{n}", tag="bank") for n in early_pairs}

            def early_matmul(a, cols, cb):
                half = cols.start // BANK
                nc.tensor.matmul(
                    k_banks[2 * a + half][:, cols.start - half * BANK : cols.stop - half * BANK],
                    lhsT=kw_sb[0][:, cb, a * P : (a + 1) * P],
                    rhs=h_bf[:, cb, cols],
                    start=(cb == 0 and cols.start % BANK == 0),
                    stop=(cb == EARLY - 1 and cols.stop % BANK == 0),
                )

            v_banks = []
            for cb in range(CB):
                for cols in PIECES:
                    in_sentence = cols.start % SENTENCE
                    nc.vector.tensor_tensor(
                        h32[cb][:, cols],
                        table_sb[cb][:].indirect(offsets[:, cols.start // TO_A_COLUMN : cols.stop // TO_A_COLUMN]),
                        pos_sb[cb][:, in_sentence : in_sentence + cols.stop - cols.start],
                        ADD,
                    )
                    nc.scalar.copy(h_bf[:, cb, cols], h32[cb][:, cols])
                nc.sync.dma_start(out[cb * P : (cb + 1) * P, :], h32[cb][:])
                if cb < EARLY:
                    for cols in PIECES:
                        for a in range(HALF_HEADS):
                            early_matmul(a, cols, cb)
                else:
                    for t in range(TB):
                        v_matmul(v_banks[t], t, 0, cb)
                if cb == EARLY - 1:
                    for n in early_pairs[:2]:
                        nc.vector.tensor_copy(k_early[n][:], k_banks[n][:])
                    for n in early_pairs[2:]:
                        nc.scalar.copy(k_early[n][:], k_banks[n][:])
                    for t in range(TB):
                        v_banks.append(psum.tile([P, BANK], F32, name=f"v_bank{t}", tag="bank"))
                        for behind in range(EARLY):
                            v_matmul(v_banks[t], t, 0, behind)
        for t in range(TB):
            add_vb(v_banks[t], t, 0)

        with (
            tc.tile_pool(name="work", bufs=2) as work,
            tc.tile_pool(name="stats", bufs=2) as stats,
            tc.tile_pool(name="flipped", bufs=1) as flipped,
            tc.tile_pool(name="results", bufs=2 * HALF_HEADS) as results,
            tc.tile_pool(name="queries", bufs=1) as queries,
        ):
            q_sb = queries.tile([P, HEADS, TOKENS], BF16, name="q_sb")

            p_tiles, pT_tiles = {}, {}

            def open_flip(n):
                return None if n is None else psum.tile([P, 2, SB, SENTENCE], BF16, name="pT_bank", tag="bank")

            def flip_block(n, pT_bank, step):
                if n is None:
                    return
                s, ib, jb = step // (SB * SB), step // SB % SB, step % SB
                nc.tensor.transpose(
                    pT_bank[:, s, ib, jb * P : (jb + 1) * P], p_tiles[n][:, s, jb, ib * P : (ib + 1) * P], ident_bf[:]
                )

            def close_flip(n, pT_bank):
                if n is None:
                    return
                pT_tiles[n] = flipped.tile([P, 2, SB, SENTENCE], BF16, name=f"pT{n}")
                nc.scalar.copy(pT_tiles[n][:], pT_bank[:])

            def project_v(t, mh, flip=None):
                bank = psum.tile([P, BANK], F32, name="v_bank", tag="bank")
                pT_bank = open_flip(flip)
                for cb in range(CB):
                    v_matmul(bank, t, mh, cb)
                    flip_block(flip, pT_bank, cb)
                add_vb(bank, t, mh)
                close_flip(flip, pT_bank)

            def project_q(n, flip=None):
                a, half = divmod(n, 2)
                bank = psum.tile([P, BANK], F32, name="q_bank", tag="bank")
                pT_bank = open_flip(flip)
                for cb in range(CB):
                    head_matmul(bank, qw_sb, n, cb, range(CB))
                    flip_block(flip, pT_bank, cb)
                close_flip(flip, pT_bank)
                nc.scalar.activation(
                    q_sb[:, a, half * BANK : (half + 1) * BANK], bank[:], IDENTITY, bias=qb_cols[:, a : a + 1]
                )

            def project_k(n):
                a, half = divmod(n, 2)
                k_cols = k_sb[:, a, half * BANK : (half + 1) * BANK]
                bank = psum.tile([P, BANK], F32, name="k_bank", tag="bank")
                blocks = range(EARLY, CB) if n < EARLY_PAIRS else range(CB)
                for cb in blocks:
                    head_matmul(bank, kw_sb, n, cb, blocks)
                if n < EARLY_PAIRS:
                    nc.vector.tensor_tensor(k_cols, bank[:], k_early[n][:], ADD)
                else:
                    nc.scalar.copy(k_cols, bank[:])

            def scores_and_softmax(n):
                a, half = divmod(n, 2)
                e = work.tile([P, 2, SB, SENTENCE], F32, name="e")
                p = work.tile([P, 2, SB, SENTENCE], BF16, name="p")
                top = stats.tile([P, 2 * SB], F32, name="top")
                shift = stats.tile([P, 2 * SB], F32, name="shift")
                total = stats.tile([P, 2 * SB], F32, name="total")
                inverse = stats.tile([P, 2 * SB], F32, name="inverse")
                for s in range(2):
                    first = half * BANK + s * SENTENCE
                    sc = psum.tile([P, SB, SENTENCE], F32, name="sc", tag="bank")
                    for jb in range(SB):
                        nc.tensor.matmul(
                            sc[:, jb, :],
                            lhsT=q_sb[:, a, first + jb * P : first + (jb + 1) * P],
                            rhs=k_sb[:, a, first : first + SENTENCE],
                            start=True,
                            stop=True,
                        )
                    of_s = slice(s * SB, (s + 1) * SB)
                    nc.vector.reduce_max(top[:, of_s], sc[:], axis=X)
                    nc.vector.tensor_scalar_mul(shift[:, of_s], top[:, of_s], -SCALE)
                    for jb in range(SB):
                        one = slice(s * SB + jb, s * SB + jb + 1)
                        nc.scalar.activation(
                            e[:, s, jb, :], sc[:, jb, :], EXP, bias=shift[:, one], scale=SCALE, accum_out=total[:, one]
                        )
                for s in range(2):
                    of_s = slice(s * SB, (s + 1) * SB)
                    nc.vector.reciprocal(inverse[:, of_s], total[:, of_s])
                    for jb in range(SB):
                        one = slice(s * SB + jb, s * SB + jb + 1)
                        nc.vector.tensor_scalar_mul(p[:, s, jb, :], e[:, s, jb, :], inverse[:, one])
                p_tiles[n] = p

            def weighted_values(heads, b):
                half, s = divmod(b, 2)
                att_banks = [psum.tile([P, SENTENCE], F32, name=f"att_bank{a}", tag="bank") for a in heads]
                for ib in range(SB):
                    for a, att_bank in zip(heads, att_banks):
                        nc.tensor.matmul(
                            att_bank[:],
                            lhsT=vT_sb[:, b * SB + ib, a * P : (a + 1) * P],
                            rhs=pT_tiles[2 * a + half][:, s, ib, :],
                            start=(ib == 0),
                            stop=(ib == SB - 1),
                        )
                for a, att_bank in zip(heads, att_banks):
                    att = results.tile([P, SENTENCE], F32, name="att")
                    if a % 2 == 0:
                        nc.scalar.copy(att[:], att_bank[:])
                    else:
                        nc.vector.tensor_copy(att[:], att_bank[:])
                    nc.sync.dma_start(
                        out[CHANNELS + a * P : CHANNELS + (a + 1) * P, b * SENTENCE : (b + 1) * SENTENCE], att[:]
                    )

            project_q(0)
            project_k(0)
            for n in range(PAIRS):
                flip = n - 2 if n >= 2 else None
                if n + 1 < PAIRS:
                    project_q(n + 1, flip)
                else:
                    project_v(0, 1, flip)
                scores_and_softmax(n)
                if n + 1 < PAIRS:
                    project_k(n + 1)
                if 2 <= n < PAIRS // 2 + 2:
                    a, half = divmod(n - 2, 2)
                    weighted_values([a], 2 * half)
                    weighted_values([a], 2 * half + 1)

            late_heads = range(HALF_HEADS, HEADS)
            project_v(1, 1, PAIRS - 2)
            project_v(2, 1)
            weighted_values(late_heads, 0)
            project_v(3, 1, PAIRS - 1)
            project_v(4, 1)
            weighted_values(late_heads, 1)
            project_v(5, 1)
            project_v(6, 1)
            project_v(7, 1)
            weighted_values(late_heads, 2)
            weighted_values(late_heads, 3)
